import numpy as np
import ml_dtypes


def mxq(x, axis, fmt="e4m3"):
    dtype, down = {"e4m3": (ml_dtypes.float8_e4m3fn, 7), "e5m2": (ml_dtypes.float8_e5m2, 14)}[fmt]
    v = np.moveaxis(np.asarray(x, np.float32).astype(ml_dtypes.bfloat16).astype(np.float64), axis, -1)
    blocks = v.reshape(v.shape[:-1] + (-1, 32))
    amax = np.abs(blocks).max(-1, keepdims=True)
    byte = np.maximum(np.where(amax > 0, np.frexp(amax)[1] - 1 + 127, 0) - down, 1)
    scale = np.exp2(byte - 127.0)
    codes = (blocks / scale).astype(np.float32).astype(dtype).astype(np.float64)
    return np.moveaxis((codes * scale).reshape(v.shape), -1, axis)


WIDE = False


def mx_kscale(k):
    if not WIDE:
        return np.ones(k)
    levels = np.array([18, -18])
    if k % 512:
        return np.exp2(np.random.permutation(np.resize(levels, k // 32))).repeat(32)
    a = np.empty((k // 512, 16))
    for p in range(k // 512):
        a[p, :8] = np.random.permutation(np.resize(levels, 8))
        for g in range(8):
            far = levels[np.abs(levels - a[p, g]) >= 10]
            a[p, g + 8] = far[np.random.randint(len(far))]
    return np.exp2(a.ravel()).repeat(32)


BF16 = ml_dtypes.bfloat16


def bf(x):
    return np.asarray(x, np.float32).astype(BF16)


def f64(x):
    return np.asarray(x).astype(np.float64)


C, F1, F2 = 512, 1024, 2048
SLOPE = 0.2
PE = 2.0 / np.sqrt(C)


def leaky_relu(v):
    return np.where(v >= 0.0, v, SLOPE * v)


def setup_inputs():
    u = mx_kscale(C)
    v = mx_kscale(F2)
    s = mx_kscale(C)
    x0 = bf(np.random.standard_normal((C, F1)))
    A0 = bf(np.random.uniform(size=(C, C)) * (np.random.uniform(size=(C, C)) < PE))
    w0 = bf(np.random.standard_normal((F1, F2)) * 2.6 / np.sqrt(F1))
    g = bf(np.random.standard_normal((C, F2)) * np.exp2(np.random.randint(-6, 1, (C, 1))) * 4.0 * u[:, None] * v[None, :])
    dis = f64(A0).sum(1) ** -0.5
    return {"x_pre": bf(f64(x0) * s[:, None]),
            "A": bf(f64(A0) / s[:, None] / u[None, :]),
            "W_gc2": bf(f64(w0) / v[None, :]),
            "dis": np.asarray(dis, np.float32),
            "grad_out": g}


def reference(x_pre, A, W_gc2, dis, grad_out):
    xf = f64(x_pre)
    df = f64(dis)[:, None]
    dz2 = df * f64(grad_out)
    dh = mxq(f64(A), 1, "e4m3") @ mxq(dz2, 0, "e5m2")
    dz1 = df * dh
    da = mxq(dz1, 1, "e5m2") @ mxq(f64(W_gc2), 1, "e4m3").T
    dx = da * np.where(xf >= 0.0, 1.0, SLOPE)
    dw = mxq(leaky_relu(xf), 0, "e4m3").T @ mxq(dz1, 0, "e5m2")
    return dx, dw

@@ -1,0 +1,303 @@
+from contextlib import ExitStack
+
+import concourse.mybir as mybir
+from concourse.masks import make_identity
+
+C, F1, F2 = 512, 1024, 2048
+SLOPE = 0.2
+FLOPS = 2 * C * C * F2 + 2 * C * F2 * F1 + 2 * C * F1 * F2
+
+F32 = mybir.dt.float32
+BF16 = mybir.dt.bfloat16
+U32 = mybir.dt.uint32
+U8 = mybir.dt.uint8
+E4M3 = mybir.dt.float8_e4m3fn_x4
+E5M2 = mybir.dt.float8_e5m2_x4
+ALU = mybir.AluOpType
+ACT = mybir.ActivationFunctionType
+
+P = 128
+PACK = 4
+NB = 512
+GRP = 4
+WGRP = 4
+STG = 6
+
+
+def tile_gcnresnet_pa_v_kernel(tc, x_pre, A, W_gc2, dis, grad_out, out_0, out_1):
+    nc = tc.nc
+    V, S = nc.vector, nc.scalar
+
+    with ExitStack() as ctx:
+        keep = ctx.enter_context(tc.tile_pool(name="keep", bufs=1))
+        work = ctx.enter_context(tc.tile_pool(name="work", bufs=1))
+        psum = ctx.enter_context(tc.psum_pool(name="psum", bufs=1))
+        ctx.enter_context(tc.manual_schedule())
+
+        def kept(name, shape, dtype):
+            return keep.tile(shape, dtype, name=name, align_bytes=64)
+
+        def ring(name, shape, dtype, bufs):
+            return work.tile(shape, dtype, name=name, tag=name, bufs=bufs, align_bytes=64)
+
+        turnstile = [0, 2]
+
+        def bank(side=None):
+            if side is None:
+                side = turnstile[0] % turnstile[1]
+                turnstile[0] = turnstile[0] + 1
+            return psum.tile([P, NB], F32, name="bank%d_" % side, tag="bank%d" % side, bufs=4)
+
+        def copy(eng, out, in_):
+            if eng is S:
+                S.copy(out=out, in_=in_)
+            else:
+                V.tensor_copy(out=out, in_=in_)
+
+        ident = kept("ident", [P, P], F32)
+        make_identity(nc, ident[:])
+
+        g_rows = grad_out.rearrange("(p j) f -> p j f", j=PACK)
+        x_rows = x_pre.rearrange("(p j) a -> p j a", j=PACK)
+        g_sb, x_sb, w_sb = {}, {}, {}
+
+        def load_g(c0, n):
+            t = kept("g%d" % c0, [P, PACK, n * NB], BF16)
+            nc.sync.dma_start(out=t[:], in_=g_rows[:, :, c0 * NB : (c0 + n) * NB])
+            for c in range(n):
+                g_sb[c0 + c] = t[:, :, c * NB : (c + 1) * NB]
+
+        def load_x(h):
+            t = kept("x%d" % h, [P, PACK, NB], BF16)
+            nc.sync.dma_start(out=t[:], in_=x_rows[:, :, h * NB : (h + 1) * NB])
+            x_sb[h] = t
+
+        def load_w(h, c0, n):
+            t = kept("w%d%d" % (h, c0), [P, 4, n * NB], BF16)
+            rows = W_gc2[h * NB : (h + 1) * NB, c0 * NB : (c0 + n) * NB]
+            nc.sync.dma_start(out=t[:], in_=rows.rearrange("(r m) f -> m r f", m=P))
+            for c in range(n):
+                w_sb[h, c0 + c] = (t, c * 256)
+
+        dis_sb = kept("dis", [P, PACK], F32)
+        a_sb = kept("a", [P, PACK, C], BF16)
+
+        def load_dis():
+            nc.sync.dma_start(out=dis_sb[:], in_=dis.rearrange("(p j) -> p j", j=PACK))
+
+        def load_a():
+            nc.sync.dma_start(out=a_sb[:], in_=A.rearrange("(m t) k -> m t k", t=PACK))
+
+        codes = {}
+        grouped = {}
+
+        def group_tile(key):
+            if key not in grouped:
+                grouped[key] = ring("wgrp" if key[0] == "w" else "grp", [P, NB * PACK], BF16, WGRP if key[0] == "w" else GRP)
+            return grouped[key]
+
+        def interleave(eng, key, src, c0=0, c1=NB):
+            dst = group_tile(key)[:, c0 * PACK : c1 * PACK]
+            copy(eng, dst.rearrange("p (c i t) -> p c t i", i=4, t=PACK),
+                 src[:, :, c0:c1].rearrange("p t (c i) -> p c t i", i=4))
+
+        def quantize(key, fmt, src=None):
+            q = kept("q_%s%d" % key, [P, NB], U32)
+            s = kept("s_%s%d" % key, [P, NB], U8)
+            V.quantize_mx(out=q[:].bitcast(fmt), scales=s[:], in_=(grouped[key] if src is None else src)[:])
+            codes[key] = (q, s, fmt)
+
+        def mx(acc, lhs, m, rhs, start, stop):
+            lq, ls, lf = codes[lhs]
+            rq, rs, rf = codes[rhs]
+            cols = slice(m * P, (m + 1) * P)
+            nc.tensor.matmul_mx(out=acc[:], lhsT=lq[:, cols].bitcast(lf), lhsT_scale=ls[:, cols],
+                                rhs=rq[:].bitcast(rf), rhs_scale=rs[:], start=start, stop=stop)
+
+        tbanks = {}
+
+        def turn(key, block):
+            for b in range(2):
+                t = bank()
+                for r in range(2):
+                    for u in range(2):
+                        nc.tensor.transpose(t[:, (2 * r + u) * P : (2 * r + u + 1) * P], block(2 * b + r, u), ident[:])
+                tbanks[key, b] = t
+
+        def turn_out(eng, key, b):
+            dst = group_tile(key)[:, b * 2 * NB : (b + 1) * 2 * NB].bitcast(F32)
+            copy(eng, dst.rearrange("p (r m u) -> p r m u", r=2, u=2),
+                 tbanks[key, b][:].rearrange("p (r u m) -> p r m u", r=2, u=2))
+
+        def turn_a():
+            words = a_sb[:].bitcast(F32)
+            turn(("a", 0), lambda r, u: words[:, r, u : C // 2 : 2])
+
+        def turn_w(h, c):
+            words = w_sb[h, c][0][:].bitcast(F32)
+            w0 = w_sb[h, c][1]
+            turn(("w", 4 * h + c), lambda r, u: words[:, r, w0 + u : w0 + 256 : 2])
+
+        dz2 = {}
+
+        def scale_g(c):
+            t = g_sb[c]
+            for j in range(PACK):
+                V.tensor_scalar(out=t[:, j, :], in0=g_sb[c][:, j, :], scalar1=dis_sb[:, j : j + 1], scalar2=None, op0=ALU.mult)
+            dz2[c] = t
+
+        dh, dz1 = {}, {}
+
+        def mm_dh(c, ts):
+            for t in ts:
+                dh[c, t] = bank()
+                mx(dh[c, t], ("a", 0), t, ("g", c), True, True)
+
+        def out_dh(eng, c, t):
+            if c not in dz1:
+                dz1[c] = ring("dz1", [P, PACK, NB], BF16, 3)
+            dst = dz1[c][:, t, :].rearrange("p (u w e) -> p u w e", u=2, e=2)
+            src = dh[c, t][:].rearrange("p (w u e) -> p u w e", u=2, e=2)
+            if eng is S:
+                S.activation(out=dst, in_=src, func=ACT.Copy, scale=dis_sb[:, t : t + 1])
+            else:
+                V.tensor_scalar(out=dst, in0=src, scalar1=dis_sb[:, t : t + 1], scalar2=None, op0=ALU.mult)
+
+        def turn_dz1(c):
+            words = dz1[c][:].bitcast(F32)
+            turn(("t", c), lambda r, u: words[:, r, u * P : (u + 1) * P])
+
+        mask, leak, hid = {}, {}, {}
+
+        def make_mask(h):
+            mask[h] = kept("mask%d" % h, [P, PACK, NB], BF16)
+            V.tensor_scalar(out=mask[h][:], in0=x_sb[h][:], scalar1=0.0, scalar2=None, op0=ALU.is_ge)
+
+        def h_low(h):
+            leak[h] = ring("leak", [P, NB * PACK], BF16, 1)
+            V.tensor_scalar(out=leak[h][:], in0=grouped["x", h][:], scalar1=SLOPE, scalar2=None, op0=ALU.mult)
+
+        def h_max(h):
+            hid[h] = ring("hid", [P, NB * PACK], BF16, 1)
+            V.tensor_tensor(out=hid[h][:], in0=grouped["x", h][:], in1=leak[h][:], op=ALU.max)
+
+        dw, stage1 = {}, {}
+
+        def mm_dw(c, s):
+            dw[c, s] = bank()
+            mx(dw[c, s], ("h", s // 4), s % 4, ("n", c), True, True)
+
+        def out_dw(eng, c, s):
+            key = (c // 2, s)
+            if key not in stage1:
+                stage1[key] = ring("stage", [P, 2 * NB], F32, STG)
+            dst = stage1[key][:, (c % 2) * NB : (c % 2 + 1) * NB]
+            copy(eng, dst.rearrange("p (w u e) -> p w u e", u=2, e=2),
+                 dw[c, s][:].rearrange("p (u w e) -> p w u e", u=2, e=2))
+
+        def store_dw(cp, s):
+            nc.sync.dma_start(out=out_1[s * P : (s + 1) * P, cp * 2 * NB : (cp + 1) * 2 * NB], in_=stage1[cp, s][:])
+
+        def out_dw2(eng, c, s):
+            key = ("two", c, s // 2)
+            if key not in stage1:
+                stage1[key] = ring("stage", [P, 2 * NB], F32, STG)
+            dst = stage1[key][:, (s % 2) * NB : (s % 2 + 1) * NB]
+            copy(eng, dst.rearrange("p (w u e) -> p w u e", u=2, e=2),
+                 dw[c, s][:].rearrange("p (u w e) -> p w u e", u=2, e=2))
+
+        def store_dw2(c, sp):
+            rows = out_1[sp * 2 * P : (sp + 1) * 2 * P, c * NB : (c + 1) * NB]
+            nc.sync.dma_start(out=rows.rearrange("(s m) f -> m s f", m=P),
+                              in_=stage1["two", c, sp][:].rearrange("p (s f) -> p s f", s=2))
+
+        da = {}
+        o_rows = out_0.rearrange("(p t) a -> p t a", t=PACK)
+
+        def mm_da(h, t, cs, side=None):
+            if (h, t) not in da:
+                da[h, t] = bank(side)
+            for c in cs:
+                mx(da[h, t], ("t", c), t, ("w", 4 * h + c), c == 0, c == 3)
+
+        def out_da(h, t):
+            st = ring("stage0", [P, NB], F32, 4)
+            V.scalar_tensor_tensor(out=st[:], in0=mask[h][:, t, :], scalar=SLOPE, in1=da[h, t][:], op0=ALU.max, op1=ALU.mult)
+            nc.sync.dma_start(out=o_rows[:, t, h * NB : (h + 1) * NB], in_=st[:])
+
+
+        def w_turn(h, c, e0=S, e1=S):
+            turn_w(h, c); turn_out(e0, ("w", 4 * h + c), 0); turn_out(e1, ("w", 4 * h + c), 1)
+
+        def t_step(c, e0=S, e1=S):
+            turn_dz1(c); turn_out(e0, ("t", c), 0); turn_out(e1, ("t", c), 1)
+
+        def dh_all(c):
+            mm_dh(c, range(4))
+            for t in range(4):
+                out_dh(S, c, t)
+
+        def dw_step(cp, s, e0=S, e1=S):
+            mm_dw(2 * cp, s); mm_dw(2 * cp + 1, s); out_dw(e0, 2 * cp, s); out_dw(e1, 2 * cp + 1, s); store_dw(cp, s)
+
+        def dw2(c, sp, e0=S, e1=S):
+            mm_dw(c, 2 * sp); mm_dw(c, 2 * sp + 1); out_dw2(e0, c, 2 * sp); out_dw2(e1, c, 2 * sp + 1); store_dw2(c, sp)
+
+        def gi(c, e=V, a=0, b=NB):
+            interleave(e, ("g", c), dz2[c], a, b)
+
+        def xi(c, e=V, a=0, b=NB):
+            interleave(e, ("x", c), x_sb[c], a, b)
+
+        def ni(c, e=V, a=0, b=NB):
+            interleave(e, ("n", c), dz1[c], a, b)
+
+        def q5(k, c):
+            quantize((k, c), E5M2)
+
+        def q4(k, c):
+            quantize((k, c), E4M3)
+
+        def hq(h):
+            quantize(("h", h), E4M3, hid[h])
+
+        load_dis(); load_g(0, 1); load_a(); load_x(0); load_g(1, 1); load_w(0, 0, 2); load_x(1); load_g(2, 2); load_w(0, 2, 2); load_w(1, 0, 2); load_w(1, 2, 2)
+        scale_g(0); gi(0, V, 0, 336); gi(0, S, 336, 512)
+        turn_a(); turn_out(S, ("a", 0), 0); turn_out(S, ("a", 0), 1)
+        q5("g", 0); xi(0, V, 0, 320); q4("a", 0); xi(0, S, 320, 512)
+        dh_all(0)
+        scale_g(1); make_mask(0); gi(1); h_low(0); q5("g", 1)
+        dh_all(1)
+        ni(0); h_max(0); q5("n", 0)
+        w_turn(0, 0)
+        t_step(0)
+        hq(0); ni(1); q4("w", 0); q5("n", 1)
+        w_turn(0, 1)
+        dw_step(0, 0); dw_step(0, 1)
+        xi(1); q5("t", 0); h_low(1); scale_g(2); h_max(1); gi(2); hq(1); q5("g", 2)
+        t_step(1)
+        dw_step(0, 2); dw_step(0, 3)
+        dh_all(2)
+        scale_g(3); q4("w", 1); gi(3); q5("t", 1); q5("g", 3)
+        w_turn(0, 2, S, V)
+        dw_step(0, 4); dw_step(0, 5)
+        ni(2); q4("w", 2); q5("n", 2)
+        dh_all(3)
+        w_turn(0, 3, V, V)
+        dw_step(0, 6); dw_step(0, 7)
+        t_step(2, V, V)
+        ni(3); q4("w", 3); q5("t", 2); q5("n", 3)
+        dw2(2, 0); dw2(2, 1)
+        t_step(3, V, V)
+        w_turn(1, 0)
+        dw2(2, 2); dw2(2, 3)
+        q5("t", 3); make_mask(1); q4("w", 4)
+        w_turn(1, 1)
+        mm_da(0, 0, range(4)); dw2(3, 0); out_da(0, 0); q4("w", 5)
+        w_turn(1, 2)
+        mm_da(0, 1, range(4)); dw2(3, 1); out_da(0, 1); q4("w", 6)
+        w_turn(1, 3)
+        mm_da(0, 2, range(4)); dw2(3, 2); out_da(0, 2); q4("w", 7)
+        mm_da(0, 3, range(4)); dw2(3, 3); out_da(0, 3)
+        for t in range(4):
+            mm_da(1, t, range(4)); out_da(1, t)

@@ -19,9 +19,9 @@ ACT = mybir.ActivationFunctionType
 P = 128
 PACK = 4
 NB = 512
-GRP = 4
+GRP = 3
 WGRP = 4
-STG = 6
+STG = 8
 
 
 def tile_gcnresnet_pa_v_kernel(tc, x_pre, A, W_gc2, dis, grad_out, out_0, out_1):
@@ -40,13 +40,16 @@ def tile_gcnresnet_pa_v_kernel(tc, x_pre, A, W_gc2, dis, grad_out, out_0, out_1)
         def ring(name, shape, dtype, bufs):
             return work.tile(shape, dtype, name=name, tag=name, bufs=bufs, align_bytes=64)
 
-        turnstile = [0, 2]
+        free_banks = list(range(8))
+        holder = {}
 
-        def bank(side=None):
-            if side is None:
-                side = turnstile[0] % turnstile[1]
-                turnstile[0] = turnstile[0] + 1
-            return psum.tile([P, NB], F32, name="bank%d_" % side, tag="bank%d" % side, bufs=4)
+        def bank(key):
+            b = free_banks.pop(0)
+            holder[key] = b
+            return psum.tile([P, NB], F32, name="bank%d_" % b, tag="bank%d" % b, bufs=1)
+
+        def release(key):
+            free_banks.append(holder[key])
 
         def copy(eng, out, in_):
             if eng is S:
@@ -93,7 +96,7 @@ def tile_gcnresnet_pa_v_kernel(tc, x_pre, A, W_gc2, dis, grad_out, out_0, out_1)
 
         def group_tile(key):
             if key not in grouped:
-                grouped[key] = ring("wgrp" if key[0] == "w" else "grp", [P, NB * PACK], BF16, WGRP if key[0] == "w" else GRP)
+                grouped[key] = ring("trn" if key[0] in ("w", "t", "a") else "grp", [P, NB * PACK], BF16, WGRP if key[0] in ("w", "t", "a") else GRP)
             return grouped[key]
 
         def interleave(eng, key, src, c0=0, c1=NB):
@@ -102,8 +105,9 @@ def tile_gcnresnet_pa_v_kernel(tc, x_pre, A, W_gc2, dis, grad_out, out_0, out_1)
                  src[:, :, c0:c1].rearrange("p t (c i) -> p c t i", i=4))
 
         def quantize(key, fmt, src=None):
-            q = kept("q_%s%d" % key, [P, NB], U32)
-            s = kept("s_%s%d" % key, [P, NB], U8)
+            n = grouped[key].shape[1] // PACK
+            q = kept("q_%s%d" % key, [P, n], U32)
+            s = kept("s_%s%d" % key, [P, n], U8)
             V.quantize_mx(out=q[:].bitcast(fmt), scales=s[:], in_=(grouped[key] if src is None else src)[:])
             codes[key] = (q, s, fmt)
 
@@ -118,7 +122,7 @@ def tile_gcnresnet_pa_v_kernel(tc, x_pre, A, W_gc2, dis, grad_out, out_0, out_1)
 
         def turn(key, block):
             for b in range(2):
-                t = bank()
+                t = bank((key, b))
                 for r in range(2):
                     for u in range(2):
                         nc.tensor.transpose(t[:, (2 * r + u) * P : (2 * r + u + 1) * P], block(2 * b + r, u), ident[:])
@@ -128,12 +132,15 @@ def tile_gcnresnet_pa_v_kernel(tc, x_pre, A, W_gc2, dis, grad_out, out_0, out_1)
             dst = group_tile(key)[:, b * 2 * NB : (b + 1) * 2 * NB].bitcast(F32)
             copy(eng, dst.rearrange("p (r m u) -> p r m u", r=2, u=2),
                  tbanks[key, b][:].rearrange("p (r u m) -> p r m u", r=2, u=2))
+            release((key, b))
 
         def turn_a():
+            grouped["a", 0] = a_sb[:].rearrange("p t k -> p (t k)")
             words = a_sb[:].bitcast(F32)
             turn(("a", 0), lambda r, u: words[:, r, u : C // 2 : 2])
 
         def turn_w(h, c):
+            grouped["w", 4 * h + c] = w_sb[h, c][0][:].rearrange("p r f -> p (r f)")
             words = w_sb[h, c][0][:].bitcast(F32)
             w0 = w_sb[h, c][1]
             turn(("w", 4 * h + c), lambda r, u: words[:, r, w0 + u : w0 + 256 : 2])
@@ -150,7 +157,7 @@ def tile_gcnresnet_pa_v_kernel(tc, x_pre, A, W_gc2, dis, grad_out, out_0, out_1)
 
         def mm_dh(c, ts):
             for t in ts:
-                dh[c, t] = bank()
+                dh[c, t] = bank(("dh", c, t))
                 mx(dh[c, t], ("a", 0), t, ("g", c), True, True)
 
         def out_dh(eng, c, t):
@@ -163,6 +170,8 @@ def tile_gcnresnet_pa_v_kernel(tc, x_pre, A, W_gc2, dis, grad_out, out_0, out_1)
             else:
                 V.tensor_scalar(out=dst, in0=src, scalar1=dis_sb[:, t : t + 1], scalar2=None, op0=ALU.mult)
 
+            release(("dh", c, t))
+
         def turn_dz1(c):
             words = dz1[c][:].bitcast(F32)
             turn(("t", c), lambda r, u: words[:, r, u * P : (u + 1) * P])
@@ -173,19 +182,30 @@ def tile_gcnresnet_pa_v_kernel(tc, x_pre, A, W_gc2, dis, grad_out, out_0, out_1)
             mask[h] = kept("mask%d" % h, [P, PACK, NB], BF16)
             V.tensor_scalar(out=mask[h][:], in0=x_sb[h][:], scalar1=0.0, scalar2=None, op0=ALU.is_ge)
 
-        def h_low(h):
-            leak[h] = ring("leak", [P, NB * PACK], BF16, 1)
-            V.tensor_scalar(out=leak[h][:], in0=grouped["x", h][:], scalar1=SLOPE, scalar2=None, op0=ALU.mult)
+        PIECES = [(0, 512), (512, 768), (768, 1024)]
 
-        def h_max(h):
-            hid[h] = ring("hid", [P, NB * PACK], BF16, 1)
-            V.tensor_tensor(out=hid[h][:], in0=grouped["x", h][:], in1=leak[h][:], op=ALU.max)
+        def x_group(eng, k):
+            a0, a1 = PIECES[k]
+            n = a1 - a0
+            grouped["x", k] = ring("grp", [P, n * PACK], BF16, GRP)
+            copy(eng, grouped["x", k][:].rearrange("p (c i t) -> p c t i", i=4, t=PACK),
+                 x_sb[a0 // NB][:, :, a0 % NB : a0 % NB + n].rearrange("p t (c i) -> p c t i", i=4))
+
+        def h_low(k):
+            n = PIECES[k][1] - PIECES[k][0]
+            leak[k] = ring("leak", [P, n * PACK], BF16, 1)
+            V.tensor_scalar(out=leak[k][:], in0=grouped["x", k][:], scalar1=SLOPE, scalar2=None, op0=ALU.mult)
+
+        def h_max(k):
+            hid[k] = grouped["x", k]
+            V.tensor_tensor(out=hid[k][:], in0=grouped["x", k][:], in1=leak[k][:], op=ALU.max)
 
         dw, stage1 = {}, {}
 
         def mm_dw(c, s):
-            dw[c, s] = bank()
-            mx(dw[c, s], ("h", s // 4), s % 4, ("n", c), True, True)
+            dw[c, s] = bank(("dw", c, s))
+            k = max(i for i in range(len(PIECES)) if PIECES[i][0] <= s * P)
+            mx(dw[c, s], ("x", k), s - PIECES[k][0] // P, ("n", c), True, True)
 
         def out_dw(eng, c, s):
             key = (c // 2, s)
@@ -194,6 +214,7 @@ def tile_gcnresnet_pa_v_kernel(tc, x_pre, A, W_gc2, dis, grad_out, out_0, out_1)
             dst = stage1[key][:, (c % 2) * NB : (c % 2 + 1) * NB]
             copy(eng, dst.rearrange("p (w u e) -> p w u e", u=2, e=2),
                  dw[c, s][:].rearrange("p (u w e) -> p w u e", u=2, e=2))
+            release(("dw", c, s))
 
         def store_dw(cp, s):
             nc.sync.dma_start(out=out_1[s * P : (s + 1) * P, cp * 2 * NB : (cp + 1) * 2 * NB], in_=stage1[cp, s][:])
@@ -205,6 +226,7 @@ def tile_gcnresnet_pa_v_kernel(tc, x_pre, A, W_gc2, dis, grad_out, out_0, out_1)
             dst = stage1[key][:, (s % 2) * NB : (s % 2 + 1) * NB]
             copy(eng, dst.rearrange("p (w u e) -> p w u e", u=2, e=2),
                  dw[c, s][:].rearrange("p (u w e) -> p w u e", u=2, e=2))
+            release(("dw", c, s))
 
         def store_dw2(c, sp):
             rows = out_1[sp * 2 * P : (sp + 1) * 2 * P, c * NB : (c + 1) * NB]
@@ -216,13 +238,14 @@ def tile_gcnresnet_pa_v_kernel(tc, x_pre, A, W_gc2, dis, grad_out, out_0, out_1)
 
         def mm_da(h, t, cs, side=None):
             if (h, t) not in da:
-                da[h, t] = bank(side)
+                da[h, t] = bank(("da", h, t))
             for c in cs:
                 mx(da[h, t], ("t", c), t, ("w", 4 * h + c), c == 0, c == 3)
 
         def out_da(h, t):
             st = ring("stage0", [P, NB], F32, 4)
             V.scalar_tensor_tensor(out=st[:], in0=mask[h][:, t, :], scalar=SLOPE, in1=da[h, t][:], op0=ALU.max, op1=ALU.mult)
+            release(("da", h, t))
             nc.sync.dma_start(out=o_rows[:, t, h * NB : (h + 1) * NB], in_=st[:])
 
 
@@ -246,8 +269,8 @@ def tile_gcnresnet_pa_v_kernel(tc, x_pre, A, W_gc2, dis, grad_out, out_0, out_1)
         def gi(c, e=V, a=0, b=NB):
             interleave(e, ("g", c), dz2[c], a, b)
 
-        def xi(c, e=V, a=0, b=NB):
-            interleave(e, ("x", c), x_sb[c], a, b)
+        def xi(c, e=V):
+            x_group(e, c)
 
         def ni(c, e=V, a=0, b=NB):
             interleave(e, ("n", c), dz1[c], a, b)
@@ -259,45 +282,75 @@ def tile_gcnresnet_pa_v_kernel(tc, x_pre, A, W_gc2, dis, grad_out, out_0, out_1)
             quantize((k, c), E4M3)
 
         def hq(h):
-            quantize(("h", h), E4M3, hid[h])
+            quantize(("x", h), E4M3)
 
-        load_dis(); load_g(0, 1); load_a(); load_x(0); load_g(1, 1); load_w(0, 0, 2); load_x(1); load_g(2, 2); load_w(0, 2, 2); load_w(1, 0, 2); load_w(1, 2, 2)
+        def dh_part(c, ts, e=S):
+            mm_dh(c, ts)
+            for t in ts:
+                out_dh(e, c, t)
+
+        def dap(h, t, cs=range(4)):
+            mm_da(h, t, cs)
+
+        def dwh(c, ss, e0=S, e1=S):
+            for s in ss:
+                mm_dw(c, s)
+            out_dw(e0, c, ss[0]); out_dw(e1, c, ss[1])
+            if c % 2:
+                for s in ss:
+                    store_dw(c // 2, s)
+
+        def wt(w, e0=S, e1=S):
+            w_turn(w // 4, w % 4, e0, e1)
+
+        def lw(w):
+            load_w(w // 4, w % 4, 1)
+        load_dis(); load_g(0, 1); load_a(); load_g(1, 1); lw(0); load_g(2, 1); load_x(0); lw(1); lw(2); lw(3); load_g(3, 1); load_x(1); lw(4); lw(5); lw(6); lw(7)
         scale_g(0); gi(0, V, 0, 336); gi(0, S, 336, 512)
         turn_a(); turn_out(S, ("a", 0), 0); turn_out(S, ("a", 0), 1)
-        q5("g", 0); xi(0, V, 0, 320); q4("a", 0); xi(0, S, 320, 512)
+        q5("g", 0); scale_g(1); gi(1); q4("a", 0); q5("g", 1)
+        wt(0)
         dh_all(0)
-        scale_g(1); make_mask(0); gi(1); h_low(0); q5("g", 1)
+        scale_g(2); gi(2); xi(0); q5("g", 2); h_low(0); ni(0); h_max(0); q5("n", 0); hq(0)
+        wt(1)
         dh_all(1)
-        ni(0); h_max(0); q5("n", 0)
-        w_turn(0, 0)
+        wt(2)
+        dh_part(2, [0, 1])
         t_step(0)
-        hq(0); ni(1); q4("w", 0); q5("n", 1)
-        w_turn(0, 1)
-        dw_step(0, 0); dw_step(0, 1)
-        xi(1); q5("t", 0); h_low(1); scale_g(2); h_max(1); gi(2); hq(1); q5("g", 2)
+        dh_part(2, [2, 3])
+        ni(1); scale_g(3); q5("n", 1); gi(3); xi(1); q5("g", 3); h_low(1); ni(2); h_max(1); q5("n", 2); hq(1)
+        wt(3)
+        dw_step(0, 0)
         t_step(1)
-        dw_step(0, 2); dw_step(0, 3)
-        dh_all(2)
-        scale_g(3); q4("w", 1); gi(3); q5("t", 1); q5("g", 3)
-        w_turn(0, 2, S, V)
-        dw_step(0, 4); dw_step(0, 5)
-        ni(2); q4("w", 2); q5("n", 2)
-        dh_all(3)
-        w_turn(0, 3, V, V)
-        dw_step(0, 6); dw_step(0, 7)
-        t_step(2, V, V)
-        ni(3); q4("w", 3); q5("t", 2); q5("n", 3)
-        dw2(2, 0); dw2(2, 1)
-        t_step(3, V, V)
-        w_turn(1, 0)
-        dw2(2, 2); dw2(2, 3)
-        q5("t", 3); make_mask(1); q4("w", 4)
-        w_turn(1, 1)
-        mm_da(0, 0, range(4)); dw2(3, 0); out_da(0, 0); q4("w", 5)
-        w_turn(1, 2)
-        mm_da(0, 1, range(4)); dw2(3, 1); out_da(0, 1); q4("w", 6)
-        w_turn(1, 3)
-        mm_da(0, 2, range(4)); dw2(3, 2); out_da(0, 2); q4("w", 7)
-        mm_da(0, 3, range(4)); dw2(3, 3); out_da(0, 3)
+        dw_step(0, 1)
+        dh_part(3, [0, 1])
+        wt(4)
+        dw_step(0, 2, V, V)
+        dh_part(3, [2, 3])
+        dw_step(0, 3, V, V)
+        t_step(2)
+        dw_step(0, 4)
+        ni(3); q5("t", 0); q5("n", 3)
+        t_step(3)
+        dw_step(0, 5, V, V)
+        wt(5)
+        dw_step(1, 0)
+        q5("t", 1); q4("w", 0); q5("t", 2); q4("w", 1)
+        dw_step(1, 1, V, V)
+        wt(6)
+        dw_step(1, 2)
+        q5("t", 3); q4("w", 2); q4("w", 3); make_mask(0)
+        wt(7)
+        dw_step(1, 3)
+        dap(0, 0); xi(2); out_da(0, 0); h_low(2); q4("w", 4); h_max(2)
+        dw_step(1, 4)
+        dap(0, 1); out_da(0, 1); hq(2); q4("w", 5)
+        dw_step(1, 5)
+        dap(0, 2); out_da(0, 2); q4("w", 6)
+        dw_step(0, 6)
+        dap(0, 3); q4("w", 7); out_da(0, 3); make_mask(1)
+        dw_step(1, 6)
         for t in range(4):
-            mm_da(1, t, range(4)); out_da(1, t)
+            dap(1, t); out_da(1, t)
+            if t < 2:
+                dw_step(t, 7)

@@ -19,9 +19,15 @@ ACT = mybir.ActivationFunctionType
 P = 128
 PACK = 4
 NB = 512
-GRP = 3
-WGRP = 4
-STG = 8
+WORDS = NB // 2
+BANKS = 8
+
+H_PIECES = ((0, 512), (512, 768), (768, 1024))
+VECTOR_SHARE = (336, 304)
+
+GROUP_BUFS = 3
+W_BUFS = 6
+STAGE_BUFS = 8
 
 
 def tile_gcnresnet_pa_v_kernel(tc, x_pre, A, W_gc2, dis, grad_out, out_0, out_1):
@@ -40,317 +46,353 @@ def tile_gcnresnet_pa_v_kernel(tc, x_pre, A, W_gc2, dis, grad_out, out_0, out_1)
         def ring(name, shape, dtype, bufs):
             return work.tile(shape, dtype, name=name, tag=name, bufs=bufs, align_bytes=64)
 
-        free_banks = list(range(8))
-        holder = {}
-
-        def bank(key):
-            b = free_banks.pop(0)
-            holder[key] = b
-            return psum.tile([P, NB], F32, name="bank%d_" % b, tag="bank%d" % b, bufs=1)
-
-        def release(key):
-            free_banks.append(holder[key])
-
         def copy(eng, out, in_):
             if eng is S:
                 S.copy(out=out, in_=in_)
             else:
                 V.tensor_copy(out=out, in_=in_)
 
+        free_banks = list(range(BANKS))
+        bank_of = {}
+        in_psum = {}
+
+        def take_bank(key):
+            b = free_banks.pop(0)
+            bank_of[key] = b
+            in_psum[key] = psum.tile([P, NB], F32, name="bank%d" % b, tag="bank%d" % b, bufs=1)
+            return in_psum[key]
+
+        def give_bank(key):
+            free_banks.append(bank_of[key])
+
         ident = kept("ident", [P, P], F32)
         make_identity(nc, ident[:])
 
-        g_rows = grad_out.rearrange("(p j) f -> p j f", j=PACK)
-        x_rows = x_pre.rearrange("(p j) a -> p j a", j=PACK)
-        g_sb, x_sb, w_sb = {}, {}, {}
-
-        def load_g(c0, n):
-            t = kept("g%d" % c0, [P, PACK, n * NB], BF16)
-            nc.sync.dma_start(out=t[:], in_=g_rows[:, :, c0 * NB : (c0 + n) * NB])
-            for c in range(n):
-                g_sb[c0 + c] = t[:, :, c * NB : (c + 1) * NB]
-
-        def load_x(h):
-            t = kept("x%d" % h, [P, PACK, NB], BF16)
-            nc.sync.dma_start(out=t[:], in_=x_rows[:, :, h * NB : (h + 1) * NB])
-            x_sb[h] = t
-
-        def load_w(h, c0, n):
-            t = kept("w%d%d" % (h, c0), [P, 4, n * NB], BF16)
-            rows = W_gc2[h * NB : (h + 1) * NB, c0 * NB : (c0 + n) * NB]
-            nc.sync.dma_start(out=t[:], in_=rows.rearrange("(r m) f -> m r f", m=P))
-            for c in range(n):
-                w_sb[h, c0 + c] = (t, c * 256)
+        warm = kept("warm", [P, 16], F32)
+        V.memset(warm[:, 0:8], 0.0)
+        S.activation(out=warm[:, 8:16], in_=warm[:, 0:8], func=ACT.Copy, scale=1.0)
 
         dis_sb = kept("dis", [P, PACK], F32)
         a_sb = kept("a", [P, PACK, C], BF16)
+        x_sb = kept("x", [P, PACK, F1], BF16)
+        g_sb = [kept("g%d" % c, [P, PACK, NB], BF16) for c in range(4)]
+        w_sb = []
+        g_rows = grad_out.rearrange("(p t) f -> p t f", t=PACK)
 
-        def load_dis():
-            nc.sync.dma_start(out=dis_sb[:], in_=dis.rearrange("(p j) -> p j", j=PACK))
+        def load_g(c):
+            nc.sync.dma_start(out=g_sb[c][:], in_=g_rows[:, :, c * NB : (c + 1) * NB])
 
-        def load_a():
-            nc.sync.dma_start(out=a_sb[:], in_=A.rearrange("(m t) k -> m t k", t=PACK))
+        def load_w(k):
+            w_sb.append(ring("w", [P, 2 * F2], BF16, W_BUFS))
+            rows = W_gc2[k * 2 * P : (k + 1) * 2 * P, :].rearrange("(m r) f -> m r f", r=2)
+            nc.sync.dma_start(out=w_sb[k][:].rearrange("p (r f) -> p r f", r=2), in_=rows)
 
-        codes = {}
+        nc.sync.dma_start(out=dis_sb[:], in_=dis.rearrange("(p t) -> p t", t=PACK))
+        load_g(0)
+        nc.sync.dma_start(out=a_sb[:], in_=A.rearrange("(p t) k -> p t k", t=PACK))
+        load_g(1)
+        load_g(2)
+        nc.sync.dma_start(out=x_sb[:], in_=x_pre.rearrange("(p t) a -> p t a", t=PACK))
+        load_w(0)
+        load_w(1)
+        load_g(3)
+        load_w(2)
+        load_w(3)
+
         grouped = {}
+        codes = {}
 
-        def group_tile(key):
+        def interleave(eng, key, src, c0, c1):
             if key not in grouped:
-                grouped[key] = ring("trn" if key[0] in ("w", "t", "a") else "grp", [P, NB * PACK], BF16, WGRP if key[0] in ("w", "t", "a") else GRP)
-            return grouped[key]
+                grouped[key] = ring("group", [P, src.shape[2] * PACK], BF16, GROUP_BUFS)
+            dst = grouped[key][:, c0 * PACK : c1 * PACK]
+            copy(
+                eng,
+                dst.rearrange("p (c i t) -> p c t i", i=4, t=PACK),
+                src[:, :, c0:c1].rearrange("p t (c i) -> p c t i", i=4),
+            )
 
-        def interleave(eng, key, src, c0=0, c1=NB):
-            dst = group_tile(key)[:, c0 * PACK : c1 * PACK]
-            copy(eng, dst.rearrange("p (c i t) -> p c t i", i=4, t=PACK),
-                 src[:, :, c0:c1].rearrange("p t (c i) -> p c t i", i=4))
-
-        def quantize(key, fmt, src=None):
+        def quantize(key, fmt, operands=1):
+            name, first = key
             n = grouped[key].shape[1] // PACK
             q = kept("q_%s%d" % key, [P, n], U32)
             s = kept("s_%s%d" % key, [P, n], U8)
-            V.quantize_mx(out=q[:].bitcast(fmt), scales=s[:], in_=(grouped[key] if src is None else src)[:])
-            codes[key] = (q, s, fmt)
+            V.quantize_mx(out=q[:].bitcast(fmt), scales=s[:], in_=grouped[key][:])
+            width = n // operands
+            for i in range(operands):
+                cols = slice(i * width, (i + 1) * width)
+                codes[name, first + i] = (q[:, cols], s[:, cols], fmt)
 
         def mx(acc, lhs, m, rhs, start, stop):
             lq, ls, lf = codes[lhs]
             rq, rs, rf = codes[rhs]
             cols = slice(m * P, (m + 1) * P)
-            nc.tensor.matmul_mx(out=acc[:], lhsT=lq[:, cols].bitcast(lf), lhsT_scale=ls[:, cols],
-                                rhs=rq[:].bitcast(rf), rhs_scale=rs[:], start=start, stop=stop)
-
-        tbanks = {}
+            nc.tensor.matmul_mx(
+                out=acc[:],
+                lhsT=lq[:, cols].bitcast(lf),
+                lhsT_scale=ls[:, cols],
+                rhs=rq.bitcast(rf),
+                rhs_scale=rs,
+                start=start,
+                stop=stop,
+            )
 
         def turn(key, block):
-            for b in range(2):
-                t = bank((key, b))
-                for r in range(2):
-                    for u in range(2):
-                        nc.tensor.transpose(t[:, (2 * r + u) * P : (2 * r + u + 1) * P], block(2 * b + r, u), ident[:])
-                tbanks[key, b] = t
+            acc = take_bank(key)
+            for r in range(2):
+                for u in range(2):
+                    q = 2 * r + u
+                    nc.tensor.transpose(acc[:, q * P : (q + 1) * P], block(r, u), ident[:])
 
-        def turn_out(eng, key, b):
-            dst = group_tile(key)[:, b * 2 * NB : (b + 1) * 2 * NB].bitcast(F32)
-            copy(eng, dst.rearrange("p (r m u) -> p r m u", r=2, u=2),
-                 tbanks[key, b][:].rearrange("p (r u m) -> p r m u", r=2, u=2))
-            release((key, b))
+        def turn_slots(name, n, words, dst):
+            for b in range(2):
+                turn((name, n, b), lambda r, u: words(2 * b + r, u))
+            for b in range(2):
+                part = dst[:, b * 2 * NB : (b + 1) * 2 * NB].bitcast(F32)
+                S.copy(
+                    out=part.rearrange("p (r m u) -> p r m u", r=2, u=2),
+                    in_=in_psum[name, n, b][:].rearrange("p (r u m) -> p r m u", r=2, u=2),
+                )
+                give_bank((name, n, b))
 
         def turn_a():
-            grouped["a", 0] = a_sb[:].rearrange("p t k -> p (t k)")
             words = a_sb[:].bitcast(F32)
-            turn(("a", 0), lambda r, u: words[:, r, u : C // 2 : 2])
-
-        def turn_w(h, c):
-            grouped["w", 4 * h + c] = w_sb[h, c][0][:].rearrange("p r f -> p (r f)")
-            words = w_sb[h, c][0][:].bitcast(F32)
-            w0 = w_sb[h, c][1]
-            turn(("w", 4 * h + c), lambda r, u: words[:, r, w0 + u : w0 + 256 : 2])
-
-        dz2 = {}
+            grouped["a", 0] = a_sb[:].rearrange("p t k -> p (t k)")
+            turn_slots("a", 0, lambda t, u: words[:, t, u:WORDS:2], grouped["a", 0])
 
         def scale_g(c):
-            t = g_sb[c]
-            for j in range(PACK):
-                V.tensor_scalar(out=t[:, j, :], in0=g_sb[c][:, j, :], scalar1=dis_sb[:, j : j + 1], scalar2=None, op0=ALU.mult)
-            dz2[c] = t
+            for t in range(PACK):
+                V.tensor_scalar(
+                    out=g_sb[c][:, t, :],
+                    in0=g_sb[c][:, t, :],
+                    scalar1=dis_sb[:, t : t + 1],
+                    scalar2=None,
+                    op0=ALU.mult,
+                )
 
-        dh, dz1 = {}, {}
+        def group_g(c):
+            interleave(V, ("g", c), g_sb[c], 0, NB)
 
-        def mm_dh(c, ts):
-            for t in ts:
-                dh[c, t] = bank(("dh", c, t))
-                mx(dh[c, t], ("a", 0), t, ("g", c), True, True)
+        def group_g_shared(c):
+            interleave(V, ("g", c), g_sb[c], 0, VECTOR_SHARE[c])
+            interleave(S, ("g", c), g_sb[c], VECTOR_SHARE[c], NB)
 
-        def out_dh(eng, c, t):
-            if c not in dz1:
-                dz1[c] = ring("dz1", [P, PACK, NB], BF16, 3)
-            dst = dz1[c][:, t, :].rearrange("p (u w e) -> p u w e", u=2, e=2)
-            src = dh[c, t][:].rearrange("p (w u e) -> p u w e", u=2, e=2)
-            if eng is S:
-                S.activation(out=dst, in_=src, func=ACT.Copy, scale=dis_sb[:, t : t + 1])
-            else:
-                V.tensor_scalar(out=dst, in0=src, scalar1=dis_sb[:, t : t + 1], scalar2=None, op0=ALU.mult)
+        dz1 = [kept("dz1_%d" % c, [P, PACK, NB], BF16) for c in range(4)]
 
-            release(("dh", c, t))
+        def make_dz1(c, slots):
+            for t in slots:
+                mx(take_bank(("dh", c, t)), ("a", 0), t, ("g", c), True, True)
+            for t in slots:
+                S.activation(
+                    out=dz1[c][:, t, :].rearrange("p (u w e) -> p u w e", u=2, e=2),
+                    in_=in_psum["dh", c, t][:].rearrange("p (w u e) -> p u w e", u=2, e=2),
+                    func=ACT.Copy,
+                    scale=dis_sb[:, t : t + 1],
+                )
+                give_bank(("dh", c, t))
+
+        def group_dz1(c):
+            interleave(V, ("n", c), dz1[c], 0, NB)
+
+        for c in (0, 2):
+            grouped["t", c] = kept("dz1t_%d" % c, [P, 2 * NB * PACK], BF16)
 
         def turn_dz1(c):
             words = dz1[c][:].bitcast(F32)
-            turn(("t", c), lambda r, u: words[:, r, u * P : (u + 1) * P])
+            e0 = (c % 2) * NB * PACK
+            dst = grouped["t", c - c % 2][:, e0 : e0 + NB * PACK]
+            turn_slots("t", c, lambda t, u: words[:, t, u * P : (u + 1) * P], dst)
 
-        mask, leak, hid = {}, {}, {}
+        def turn_w(k, c0, eng=S):
+            words = w_sb[k][:].bitcast(F32)
+            key = ("w", 4 * (k // 2) + c0)
+            for c in (c0, c0 + 1):
+                w0 = c * WORDS
+                turn(
+                    ("w", k, c),
+                    lambda r, u: words[:, r * F1 + w0 + u : r * F1 + w0 + WORDS : 2],
+                )
+            if key not in grouped:
+                grouped[key] = ring("w", [P, 2 * F2], BF16, W_BUFS)
+            for c in (c0, c0 + 1):
+                e0 = (c - c0) * NB * PACK + (k % 2) * 2 * NB
+                part = grouped[key][:, e0 : e0 + 2 * NB].bitcast(F32)
+                copy(
+                    eng,
+                    part.rearrange("p (m r u) -> p m r u", r=2, u=2),
+                    in_psum["w", k, c][:].rearrange("p (r u m) -> p m r u", r=2, u=2),
+                )
+                give_bank(("w", k, c))
 
-        def make_mask(h):
-            mask[h] = kept("mask%d" % h, [P, PACK, NB], BF16)
-            V.tensor_scalar(out=mask[h][:], in0=x_sb[h][:], scalar1=0.0, scalar2=None, op0=ALU.is_ge)
+        leak = {}
 
-        PIECES = [(0, 512), (512, 768), (768, 1024)]
+        def group_x(i):
+            a0, a1 = H_PIECES[i]
+            interleave(V, ("h", i), x_sb[:, :, a0:a1], 0, a1 - a0)
 
-        def x_group(eng, k):
-            a0, a1 = PIECES[k]
-            n = a1 - a0
-            grouped["x", k] = ring("grp", [P, n * PACK], BF16, GRP)
-            copy(eng, grouped["x", k][:].rearrange("p (c i t) -> p c t i", i=4, t=PACK),
-                 x_sb[a0 // NB][:, :, a0 % NB : a0 % NB + n].rearrange("p t (c i) -> p c t i", i=4))
+        def h_leak(i):
+            leak[i] = ring("leak", list(grouped["h", i].shape), BF16, 1)
+            V.tensor_scalar(
+                out=leak[i][:], in0=grouped["h", i][:], scalar1=SLOPE, scalar2=None, op0=ALU.mult
+            )
 
-        def h_low(k):
-            n = PIECES[k][1] - PIECES[k][0]
-            leak[k] = ring("leak", [P, n * PACK], BF16, 1)
-            V.tensor_scalar(out=leak[k][:], in0=grouped["x", k][:], scalar1=SLOPE, scalar2=None, op0=ALU.mult)
+        def h_max(i):
+            V.tensor_tensor(
+                out=grouped["h", i][:], in0=grouped["h", i][:], in1=leak[i][:], op=ALU.max
+            )
 
-        def h_max(k):
-            hid[k] = grouped["x", k]
-            V.tensor_tensor(out=hid[k][:], in0=grouped["x", k][:], in1=leak[k][:], op=ALU.max)
+        staged = {}
 
-        dw, stage1 = {}, {}
+        def dw_mul(c, s):
+            i = max(n for n in range(len(H_PIECES)) if H_PIECES[n][0] <= s * P)
+            m = s - H_PIECES[i][0] // P
+            mx(take_bank(("dw", c, s)), ("h", i), m, ("n", c), True, True)
 
-        def mm_dw(c, s):
-            dw[c, s] = bank(("dw", c, s))
-            k = max(i for i in range(len(PIECES)) if PIECES[i][0] <= s * P)
-            mx(dw[c, s], ("x", k), s - PIECES[k][0] // P, ("n", c), True, True)
-
-        def out_dw(eng, c, s):
+        def dw_out(eng, c, s):
             key = (c // 2, s)
-            if key not in stage1:
-                stage1[key] = ring("stage", [P, 2 * NB], F32, STG)
-            dst = stage1[key][:, (c % 2) * NB : (c % 2 + 1) * NB]
-            copy(eng, dst.rearrange("p (w u e) -> p w u e", u=2, e=2),
-                 dw[c, s][:].rearrange("p (u w e) -> p w u e", u=2, e=2))
-            release(("dw", c, s))
+            if key not in staged:
+                staged[key] = ring("stage", [P, 2 * NB], F32, STAGE_BUFS)
+            dst = staged[key][:, (c % 2) * NB : (c % 2 + 1) * NB]
+            copy(
+                eng,
+                dst.rearrange("p (w u e) -> p w u e", u=2, e=2),
+                in_psum["dw", c, s][:].rearrange("p (u w e) -> p w u e", u=2, e=2),
+            )
+            give_bank(("dw", c, s))
 
-        def store_dw(cp, s):
-            nc.sync.dma_start(out=out_1[s * P : (s + 1) * P, cp * 2 * NB : (cp + 1) * 2 * NB], in_=stage1[cp, s][:])
+        def dw_store(pair, s):
+            cols = slice(pair * 2 * NB, (pair + 1) * 2 * NB)
+            nc.sync.dma_start(out=out_1[s * P : (s + 1) * P, cols], in_=staged[pair, s][:])
 
-        def out_dw2(eng, c, s):
-            key = ("two", c, s // 2)
-            if key not in stage1:
-                stage1[key] = ring("stage", [P, 2 * NB], F32, STG)
-            dst = stage1[key][:, (s % 2) * NB : (s % 2 + 1) * NB]
-            copy(eng, dst.rearrange("p (w u e) -> p w u e", u=2, e=2),
-                 dw[c, s][:].rearrange("p (u w e) -> p w u e", u=2, e=2))
-            release(("dw", c, s))
+        def dw(pair, s, eng=S):
+            chunks = (2 * pair, 2 * pair + 1)
+            for c in chunks:
+                dw_mul(c, s)
+            for c in chunks:
+                dw_out(eng, c, s)
+            dw_store(pair, s)
 
-        def store_dw2(c, sp):
-            rows = out_1[sp * 2 * P : (sp + 1) * 2 * P, c * NB : (c + 1) * NB]
-            nc.sync.dma_start(out=rows.rearrange("(s m) f -> m s f", m=P),
-                              in_=stage1["two", c, sp][:].rearrange("p (s f) -> p s f", s=2))
+        def dw_chunk(c, slices):
+            for s in slices:
+                dw_mul(c, s)
+            for s in slices:
+                dw_out(S, c, s)
 
-        da = {}
+        positive = {}
         o_rows = out_0.rearrange("(p t) a -> p t a", t=PACK)
 
-        def mm_da(h, t, cs, side=None):
-            if (h, t) not in da:
-                da[h, t] = bank(("da", h, t))
-            for c in cs:
-                mx(da[h, t], ("t", c), t, ("w", 4 * h + c), c == 0, c == 3)
+        def mark_positive(h):
+            positive[h] = kept("positive%d" % h, [P, PACK, NB], BF16)
+            V.tensor_scalar(
+                out=positive[h][:],
+                in0=x_sb[:, :, h * NB : (h + 1) * NB],
+                scalar1=0.0,
+                scalar2=None,
+                op0=ALU.is_ge,
+            )
 
-        def out_da(h, t):
-            st = ring("stage0", [P, NB], F32, 4)
-            V.scalar_tensor_tensor(out=st[:], in0=mask[h][:, t, :], scalar=SLOPE, in1=da[h, t][:], op0=ALU.max, op1=ALU.mult)
-            release(("da", h, t))
+        def dx(h, t):
+            acc = take_bank(("dx", h, t))
+            for c in range(4):
+                mx(acc, ("t", c), t, ("w", 4 * h + c), c == 0, c == 3)
+            st = ring("stage", [P, NB], F32, STAGE_BUFS)
+            V.scalar_tensor_tensor(
+                out=st[:],
+                in0=positive[h][:, t, :],
+                scalar=SLOPE,
+                in1=acc[:],
+                op0=ALU.max,
+                op1=ALU.mult,
+            )
+            give_bank(("dx", h, t))
             nc.sync.dma_start(out=o_rows[:, t, h * NB : (h + 1) * NB], in_=st[:])
 
 
-        def w_turn(h, c, e0=S, e1=S):
-            turn_w(h, c); turn_out(e0, ("w", 4 * h + c), 0); turn_out(e1, ("w", 4 * h + c), 1)
+        scale_g(0)
+        group_g_shared(0)
+        turn_a()
+        quantize(("g", 0), E5M2)
+        scale_g(1)
+        group_g_shared(1)
+        quantize(("a", 0), E4M3)
+        scale_g(2)
+        quantize(("g", 1), E5M2)
 
-        def t_step(c, e0=S, e1=S):
-            turn_dz1(c); turn_out(e0, ("t", c), 0); turn_out(e1, ("t", c), 1)
+        make_dz1(0, range(4))
+        group_g(2)
+        group_x(0)
+        quantize(("g", 2), E5M2)
+        h_leak(0)
+        group_dz1(0)
+        h_max(0)
+        quantize(("n", 0), E5M2)
+        quantize(("h", 0), E4M3)
+        make_dz1(1, range(4))
+        turn_w(0, 0)
+        make_dz1(2, (0, 1))
+        turn_w(0, 2)
+        make_dz1(2, (2, 3))
+        group_dz1(1)
+        scale_g(3)
+        quantize(("n", 1), E5M2)
+        group_g(3)
+        group_x(1)
+        quantize(("g", 3), E5M2)
+        h_leak(1)
+        group_dz1(2)
+        h_max(1)
+        quantize(("n", 2), E5M2)
+        quantize(("h", 1), E4M3)
 
-        def dh_all(c):
-            mm_dh(c, range(4))
-            for t in range(4):
-                out_dh(S, c, t)
+        dw_chunk(0, (0, 1))
+        turn_w(1, 0)
+        dw_chunk(1, (0, 1))
+        dw_store(0, 0)
+        dw_store(0, 1)
+        turn_dz1(0)
+        dw(0, 2)
+        make_dz1(3, range(4))
+        turn_dz1(1)
 
-        def dw_step(cp, s, e0=S, e1=S):
-            mm_dw(2 * cp, s); mm_dw(2 * cp + 1, s); out_dw(e0, 2 * cp, s); out_dw(e1, 2 * cp + 1, s); store_dw(cp, s)
+        dw(0, 3, V)
+        dw(0, 4, V)
+        dw(0, 5)
+        turn_w(1, 2)
+        group_dz1(3)
+        group_x(2)
+        quantize(("n", 3), E5M2)
+        h_leak(2)
+        turn_dz1(2)
+        turn_dz1(3)
+        dw(1, 0, V)
+        h_max(2)
+        dw(1, 1, V)
+        dw(1, 2)
+        turn_w(2, 0)
+        dw(1, 3)
 
-        def dw2(c, sp, e0=S, e1=S):
-            mm_dw(c, 2 * sp); mm_dw(c, 2 * sp + 1); out_dw2(e0, c, 2 * sp); out_dw2(e1, c, 2 * sp + 1); store_dw2(c, sp)
+        quantize(("h", 2), E4M3)
+        quantize(("t", 0), E5M2, 2)
+        quantize(("w", 0), E4M3, 2)
+        quantize(("t", 2), E5M2, 2)
+        quantize(("w", 2), E4M3, 2)
+        dw(1, 4)
+        turn_w(3, 0)
+        dw(1, 5)
+        turn_w(2, 2, V)
+        dw(0, 6)
+        mark_positive(0)
+        turn_w(3, 2)
 
-        def gi(c, e=V, a=0, b=NB):
-            interleave(e, ("g", c), dz2[c], a, b)
-
-        def xi(c, e=V):
-            x_group(e, c)
-
-        def ni(c, e=V, a=0, b=NB):
-            interleave(e, ("n", c), dz1[c], a, b)
-
-        def q5(k, c):
-            quantize((k, c), E5M2)
-
-        def q4(k, c):
-            quantize((k, c), E4M3)
-
-        def hq(h):
-            quantize(("x", h), E4M3)
-
-        def dh_part(c, ts, e=S):
-            mm_dh(c, ts)
-            for t in ts:
-                out_dh(e, c, t)
-
-        def dap(h, t, cs=range(4)):
-            mm_da(h, t, cs)
-
-        def dwh(c, ss, e0=S, e1=S):
-            for s in ss:
-                mm_dw(c, s)
-            out_dw(e0, c, ss[0]); out_dw(e1, c, ss[1])
-            if c % 2:
-                for s in ss:
-                    store_dw(c // 2, s)
-
-        def wt(w, e0=S, e1=S):
-            w_turn(w // 4, w % 4, e0, e1)
-
-        def lw(w):
-            load_w(w // 4, w % 4, 1)
-        load_dis(); load_g(0, 1); load_a(); load_g(1, 1); lw(0); load_g(2, 1); load_x(0); lw(1); lw(2); lw(3); load_g(3, 1); load_x(1); lw(4); lw(5); lw(6); lw(7)
-        scale_g(0); gi(0, V, 0, 336); gi(0, S, 336, 512)
-        turn_a(); turn_out(S, ("a", 0), 0); turn_out(S, ("a", 0), 1)
-        q5("g", 0); scale_g(1); gi(1); q4("a", 0); q5("g", 1)
-        wt(0)
-        dh_all(0)
-        scale_g(2); gi(2); xi(0); q5("g", 2); h_low(0); ni(0); h_max(0); q5("n", 0); hq(0)
-        wt(1)
-        dh_all(1)
-        wt(2)
-        dh_part(2, [0, 1])
-        t_step(0)
-        dh_part(2, [2, 3])
-        ni(1); scale_g(3); q5("n", 1); gi(3); xi(1); q5("g", 3); h_low(1); ni(2); h_max(1); q5("n", 2); hq(1)
-        wt(3)
-        dw_step(0, 0)
-        t_step(1)
-        dw_step(0, 1)
-        dh_part(3, [0, 1])
-        wt(4)
-        dw_step(0, 2, V, V)
-        dh_part(3, [2, 3])
-        dw_step(0, 3, V, V)
-        t_step(2)
-        dw_step(0, 4)
-        ni(3); q5("t", 0); q5("n", 3)
-        t_step(3)
-        dw_step(0, 5, V, V)
-        wt(5)
-        dw_step(1, 0)
-        q5("t", 1); q4("w", 0); q5("t", 2); q4("w", 1)
-        dw_step(1, 1, V, V)
-        wt(6)
-        dw_step(1, 2)
-        q5("t", 3); q4("w", 2); q4("w", 3); make_mask(0)
-        wt(7)
-        dw_step(1, 3)
-        dap(0, 0); xi(2); out_da(0, 0); h_low(2); q4("w", 4); h_max(2)
-        dw_step(1, 4)
-        dap(0, 1); out_da(0, 1); hq(2); q4("w", 5)
-        dw_step(1, 5)
-        dap(0, 2); out_da(0, 2); q4("w", 6)
-        dw_step(0, 6)
-        dap(0, 3); q4("w", 7); out_da(0, 3); make_mask(1)
-        dw_step(1, 6)
-        for t in range(4):
-            dap(1, t); out_da(1, t)
-            if t < 2:
-                dw_step(t, 7)
+        dx(0, 0)
+        quantize(("w", 4), E4M3, 2)
+        dw(1, 6)
+        dx(0, 1)
+        quantize(("w", 6), E4M3, 2)
+        dw(0, 7)
+        dx(0, 2)
+        mark_positive(1)
+        dw(1, 7)
+        dx(0, 3)
+        for t in range(PACK):
+            dx(1, t)

from contextlib import ExitStack

import concourse.mybir as mybir
from concourse.masks import make_identity

C, F1, F2 = 512, 1024, 2048
SLOPE = 0.2
FLOPS = 2 * C * C * F2 + 2 * C * F2 * F1 + 2 * C * F1 * F2

F32 = mybir.dt.float32
BF16 = mybir.dt.bfloat16
U32 = mybir.dt.uint32
U8 = mybir.dt.uint8
E4M3 = mybir.dt.float8_e4m3fn_x4
E5M2 = mybir.dt.float8_e5m2_x4
ALU = mybir.AluOpType
ACT = mybir.ActivationFunctionType

P = 128
PACK = 4
NB = 512
WORDS = NB // 2
BANKS = 8

H_PIECES = ((0, 512), (512, 768), (768, 1024))
VECTOR_SHARE = (336, 304)

GROUP_BUFS = 3
W_BUFS = 6
STAGE_BUFS = 8


def tile_gcnresnet_pa_v_kernel(tc, x_pre, A, W_gc2, dis, grad_out, out_0, out_1):
    nc = tc.nc
    V, S = nc.vector, nc.scalar

    with ExitStack() as ctx:
        keep = ctx.enter_context(tc.tile_pool(name="keep", bufs=1))
        work = ctx.enter_context(tc.tile_pool(name="work", bufs=1))
        psum = ctx.enter_context(tc.psum_pool(name="psum", bufs=1))
        ctx.enter_context(tc.manual_schedule())

        def kept(name, shape, dtype):
            return keep.tile(shape, dtype, name=name, align_bytes=64)

        def ring(name, shape, dtype, bufs):
            return work.tile(shape, dtype, name=name, tag=name, bufs=bufs, align_bytes=64)

        def copy(eng, out, in_):
            if eng is S:
                S.copy(out=out, in_=in_)
            else:
                V.tensor_copy(out=out, in_=in_)

        free_banks = list(range(BANKS))
        bank_of = {}
        in_psum = {}

        def take_bank(key):
            b = free_banks.pop(0)
            bank_of[key] = b
            in_psum[key] = psum.tile([P, NB], F32, name="bank%d" % b, tag="bank%d" % b, bufs=1)
            return in_psum[key]

        def give_bank(key):
            free_banks.append(bank_of[key])

        ident = kept("ident", [P, P], F32)
        make_identity(nc, ident[:])

        warm = kept("warm", [P, 16], F32)
        V.memset(warm[:, 0:8], 0.0)
        S.activation(out=warm[:, 8:16], in_=warm[:, 0:8], func=ACT.Copy, scale=1.0)

        dis_sb = kept("dis", [P, PACK], F32)
        a_sb = kept("a", [P, PACK, C], BF16)
        x_sb = kept("x", [P, PACK, F1], BF16)
        g_sb = [kept("g%d" % c, [P, PACK, NB], BF16) for c in range(4)]
        w_sb = []
        g_rows = grad_out.rearrange("(p t) f -> p t f", t=PACK)

        def load_g(c):
            nc.sync.dma_start(out=g_sb[c][:], in_=g_rows[:, :, c * NB : (c + 1) * NB])

        def load_w(k):
            w_sb.append(ring("w", [P, 2 * F2], BF16, W_BUFS))
            rows = W_gc2[k * 2 * P : (k + 1) * 2 * P, :].rearrange("(m r) f -> m r f", r=2)
            nc.sync.dma_start(out=w_sb[k][:].rearrange("p (r f) -> p r f", r=2), in_=rows)

        nc.sync.dma_start(out=dis_sb[:], in_=dis.rearrange("(p t) -> p t", t=PACK))
        load_g(0)
        nc.sync.dma_start(out=a_sb[:], in_=A.rearrange("(p t) k -> p t k", t=PACK))
        load_g(1)
        load_g(2)
        nc.sync.dma_start(out=x_sb[:], in_=x_pre.rearrange("(p t) a -> p t a", t=PACK))
        load_w(0)
        load_w(1)
        load_g(3)
        load_w(2)
        load_w(3)

        grouped = {}
        codes = {}

        def interleave(eng, key, src, c0, c1):
            if key not in grouped:
                grouped[key] = ring("group", [P, src.shape[2] * PACK], BF16, GROUP_BUFS)
            dst = grouped[key][:, c0 * PACK : c1 * PACK]
            copy(
                eng,
                dst.rearrange("p (c i t) -> p c t i", i=4, t=PACK),
                src[:, :, c0:c1].rearrange("p t (c i) -> p c t i", i=4),
            )

        def quantize(key, fmt, operands=1):
            name, first = key
            n = grouped[key].shape[1] // PACK
            q = kept("q_%s%d" % key, [P, n], U32)
            s = kept("s_%s%d" % key, [P, n], U8)
            V.quantize_mx(out=q[:].bitcast(fmt), scales=s[:], in_=grouped[key][:])
            width = n // operands
            for i in range(operands):
                cols = slice(i * width, (i + 1) * width)
                codes[name, first + i] = (q[:, cols], s[:, cols], fmt)

        def mx(acc, lhs, m, rhs, start, stop):
            lq, ls, lf = codes[lhs]
            rq, rs, rf = codes[rhs]
            cols = slice(m * P, (m + 1) * P)
            nc.tensor.matmul_mx(
                out=acc[:],
                lhsT=lq[:, cols].bitcast(lf),
                lhsT_scale=ls[:, cols],
                rhs=rq.bitcast(rf),
                rhs_scale=rs,
                start=start,
                stop=stop,
            )

        def turn(key, block):
            acc = take_bank(key)
            for r in range(2):
                for u in range(2):
                    q = 2 * r + u
                    nc.tensor.transpose(acc[:, q * P : (q + 1) * P], block(r, u), ident[:])

        def turn_slots(name, n, words, dst):
            for b in range(2):
                turn((name, n, b), lambda r, u: words(2 * b + r, u))
            for b in range(2):
                part = dst[:, b * 2 * NB : (b + 1) * 2 * NB].bitcast(F32)
                S.copy(
                    out=part.rearrange("p (r m u) -> p r m u", r=2, u=2),
                    in_=in_psum[name, n, b][:].rearrange("p (r u m) -> p r m u", r=2, u=2),
                )
                give_bank((name, n, b))

        def turn_a():
            words = a_sb[:].bitcast(F32)
            grouped["a", 0] = a_sb[:].rearrange("p t k -> p (t k)")
            turn_slots("a", 0, lambda t, u: words[:, t, u:WORDS:2], grouped["a", 0])

        def scale_g(c):
            for t in range(PACK):
                V.tensor_scalar(
                    out=g_sb[c][:, t, :],
                    in0=g_sb[c][:, t, :],
                    scalar1=dis_sb[:, t : t + 1],
                    scalar2=None,
                    op0=ALU.mult,
                )

        def group_g(c):
            interleave(V, ("g", c), g_sb[c], 0, NB)

        def group_g_shared(c):
            interleave(V, ("g", c), g_sb[c], 0, VECTOR_SHARE[c])
            interleave(S, ("g", c), g_sb[c], VECTOR_SHARE[c], NB)

        dz1 = [kept("dz1_%d" % c, [P, PACK, NB], BF16) for c in range(4)]

        def make_dz1(c, slots):
            for t in slots:
                mx(take_bank(("dh", c, t)), ("a", 0), t, ("g", c), True, True)
            for t in slots:
                S.activation(
                    out=dz1[c][:, t, :].rearrange("p (u w e) -> p u w e", u=2, e=2),
                    in_=in_psum["dh", c, t][:].rearrange("p (w u e) -> p u w e", u=2, e=2),
                    func=ACT.Copy,
                    scale=dis_sb[:, t : t + 1],
                )
                give_bank(("dh", c, t))

        def group_dz1(c):
            interleave(V, ("n", c), dz1[c], 0, NB)

        for c in (0, 2):
            grouped["t", c] = kept("dz1t_%d" % c, [P, 2 * NB * PACK], BF16)

        def turn_dz1(c):
            words = dz1[c][:].bitcast(F32)
            e0 = (c % 2) * NB * PACK
            dst = grouped["t", c - c % 2][:, e0 : e0 + NB * PACK]
            turn_slots("t", c, lambda t, u: words[:, t, u * P : (u + 1) * P], dst)

        def turn_w(k, c0, eng=S):
            words = w_sb[k][:].bitcast(F32)
            key = ("w", 4 * (k // 2) + c0)
            for c in (c0, c0 + 1):
                w0 = c * WORDS
                turn(
                    ("w", k, c),
                    lambda r, u: words[:, r * F1 + w0 + u : r * F1 + w0 + WORDS : 2],
                )
            if key not in grouped:
                grouped[key] = ring("w", [P, 2 * F2], BF16, W_BUFS)
            for c in (c0, c0 + 1):
                e0 = (c - c0) * NB * PACK + (k % 2) * 2 * NB
                part = grouped[key][:, e0 : e0 + 2 * NB].bitcast(F32)
                copy(
                    eng,
                    part.rearrange("p (m r u) -> p m r u", r=2, u=2),
                    in_psum["w", k, c][:].rearrange("p (r u m) -> p m r u", r=2, u=2),
                )
                give_bank(("w", k, c))

        leak = {}

        def group_x(i):
            a0, a1 = H_PIECES[i]
            interleave(V, ("h", i), x_sb[:, :, a0:a1], 0, a1 - a0)

        def h_leak(i):
            leak[i] = ring("leak", list(grouped["h", i].shape), BF16, 1)
            V.tensor_scalar(
                out=leak[i][:], in0=grouped["h", i][:], scalar1=SLOPE, scalar2=None, op0=ALU.mult
            )

        def h_max(i):
            V.tensor_tensor(
                out=grouped["h", i][:], in0=grouped["h", i][:], in1=leak[i][:], op=ALU.max
            )

        staged = {}

        def dw_mul(c, s):
            i = max(n for n in range(len(H_PIECES)) if H_PIECES[n][0] <= s * P)
            m = s - H_PIECES[i][0] // P
            mx(take_bank(("dw", c, s)), ("h", i), m, ("n", c), True, True)

        def dw_out(eng, c, s):
            key = (c // 2, s)
            if key not in staged:
                staged[key] = ring("stage", [P, 2 * NB], F32, STAGE_BUFS)
            dst = staged[key][:, (c % 2) * NB : (c % 2 + 1) * NB]
            copy(
                eng,
                dst.rearrange("p (w u e) -> p w u e", u=2, e=2),
                in_psum["dw", c, s][:].rearrange("p (u w e) -> p w u e", u=2, e=2),
            )
            give_bank(("dw", c, s))

        def dw_store(pair, s):
            cols = slice(pair * 2 * NB, (pair + 1) * 2 * NB)
            nc.sync.dma_start(out=out_1[s * P : (s + 1) * P, cols], in_=staged[pair, s][:])

        def dw(pair, s, eng=S):
            chunks = (2 * pair, 2 * pair + 1)
            for c in chunks:
                dw_mul(c, s)
            for c in chunks:
                dw_out(eng, c, s)
            dw_store(pair, s)

        def dw_chunk(c, slices):
            for s in slices:
                dw_mul(c, s)
            for s in slices:
                dw_out(S, c, s)

        positive = {}
        o_rows = out_0.rearrange("(p t) a -> p t a", t=PACK)

        def mark_positive(h):
            positive[h] = kept("positive%d" % h, [P, PACK, NB], BF16)
            V.tensor_scalar(
                out=positive[h][:],
                in0=x_sb[:, :, h * NB : (h + 1) * NB],
                scalar1=0.0,
                scalar2=None,
                op0=ALU.is_ge,
            )

        def dx(h, t):
            acc = take_bank(("dx", h, t))
            for c in range(4):
                mx(acc, ("t", c), t, ("w", 4 * h + c), c == 0, c == 3)
            st = ring("stage", [P, NB], F32, STAGE_BUFS)
            V.scalar_tensor_tensor(
                out=st[:],
                in0=positive[h][:, t, :],
                scalar=SLOPE,
                in1=acc[:],
                op0=ALU.max,
                op1=ALU.mult,
            )
            give_bank(("dx", h, t))
            nc.sync.dma_start(out=o_rows[:, t, h * NB : (h + 1) * NB], in_=st[:])


        scale_g(0)
        group_g_shared(0)
        turn_a()
        quantize(("g", 0), E5M2)
        scale_g(1)
        group_g_shared(1)
        quantize(("a", 0), E4M3)
        scale_g(2)
        quantize(("g", 1), E5M2)

        make_dz1(0, range(4))
        group_g(2)
        group_x(0)
        quantize(("g", 2), E5M2)
        h_leak(0)
        group_dz1(0)
        h_max(0)
        quantize(("n", 0), E5M2)
        quantize(("h", 0), E4M3)
        make_dz1(1, range(4))
        turn_w(0, 0)
        make_dz1(2, (0, 1))
        turn_w(0, 2)
        make_dz1(2, (2, 3))
        group_dz1(1)
        scale_g(3)
        quantize(("n", 1), E5M2)
        group_g(3)
        group_x(1)
        quantize(("g", 3), E5M2)
        h_leak(1)
        group_dz1(2)
        h_max(1)
        quantize(("n", 2), E5M2)
        quantize(("h", 1), E4M3)

        dw_chunk(0, (0, 1))
        turn_w(1, 0)
        dw_chunk(1, (0, 1))
        dw_store(0, 0)
        dw_store(0, 1)
        turn_dz1(0)
        dw(0, 2)
        make_dz1(3, range(4))
        turn_dz1(1)

        dw(0, 3, V)
        dw(0, 4, V)
        dw(0, 5)
        turn_w(1, 2)
        group_dz1(3)
        group_x(2)
        quantize(("n", 3), E5M2)
        h_leak(2)
        turn_dz1(2)
        turn_dz1(3)
        dw(1, 0, V)
        h_max(2)
        dw(1, 1, V)
        dw(1, 2)
        turn_w(2, 0)
        dw(1, 3)

        quantize(("h", 2), E4M3)
        quantize(("t", 0), E5M2, 2)
        quantize(("w", 0), E4M3, 2)
        quantize(("t", 2), E5M2, 2)
        quantize(("w", 2), E4M3, 2)
        dw(1, 4)
        turn_w(3, 0)
        dw(1, 5)
        turn_w(2, 2, V)
        dw(0, 6)
        mark_positive(0)
        turn_w(3, 2)

        dx(0, 0)
        quantize(("w", 4), E4M3, 2)
        dw(1, 6)
        dx(0, 1)
        quantize(("w", 6), E4M3, 2)
        dw(0, 7)
        dx(0, 2)
        mark_positive(1)
        dw(1, 7)
        dx(0, 3)
        for t in range(PACK):
            dx(1, t)
